import numpy as np
import ml_dtypes


def mxq(x, axis, fmt="e4m3"):
    dtype, down = {"e4m3": (ml_dtypes.float8_e4m3fn, 7), "e5m2": (ml_dtypes.float8_e5m2, 14)}[fmt]
    v = np.moveaxis(np.asarray(x, np.float32).astype(ml_dtypes.bfloat16).astype(np.float64), axis, -1)
    blocks = v.reshape(v.shape[:-1] + (-1, 32))
    amax = np.abs(blocks).max(-1, keepdims=True)
    byte = np.maximum(np.where(amax > 0, np.frexp(amax)[1] - 1 + 127, 0) - down, 1)
    scale = np.exp2(byte - 127.0)
    codes = (blocks / scale).astype(np.float32).astype(dtype).astype(np.float64)
    return np.moveaxis((codes * scale).reshape(v.shape), -1, axis)


WIDE = False


def mx_kscale(k):
    if not WIDE:
        return np.ones(k)
    levels = np.array([30, -30])
    if k % 512:
        return np.exp2(np.random.permutation(np.resize(levels, k // 32))).repeat(32)
    a = np.empty((k // 512, 16))
    for p in range(k // 512):
        a[p, :8] = np.random.permutation(np.resize(levels, 8))
        for g in range(8):
            far = levels[np.abs(levels - a[p, g]) >= 10]
            a[p, g + 8] = far[np.random.randint(len(far))]
    return np.exp2(a.ravel()).repeat(32)


BF16 = ml_dtypes.bfloat16


def bf(x):
    return np.asarray(x, np.float32).astype(BF16)


def f64(x):
    return np.asarray(x).astype(np.float64)


B, N, DIM, H, DH, PD = 2, 1024, 1024, 16, 64, 2
E = H * DH
ROT = DH // PD
INV_MIN_FREQ = 2.0 ** 6


def rot_freqs(t):
    inv_freq = 1.0 / (10000.0 ** (np.arange(0, ROT, 2) / ROT))
    f = (t * INV_MIN_FREQ)[..., None] * inv_freq
    return np.concatenate([f, f], axis=-1)


def rotate_half(x):
    x1, x2 = np.split(x, 2, axis=-1)
    return np.concatenate([-x2, x1], axis=-1)


def apply_rotary(t, freqs):
    return t * np.cos(freqs) + rotate_half(t) * np.sin(freqs)


def rope_2d(t, pos):
    fx = rot_freqs(pos[..., 0])[:, None]
    fy = rot_freqs(pos[..., 1])[:, None]
    return np.concatenate([apply_rotary(t[..., :ROT], fx), apply_rotary(t[..., ROT:], fy)], axis=-1)


def setup_inputs():
    s = mx_kscale(DIM)
    return {"u_x": bf(np.random.standard_normal((B, N, DIM)) * s),
            "pos_x": bf(np.random.uniform(size=(1, N, PD))),
            "Wq": bf(np.random.standard_normal((E, DIM)) / np.sqrt(DIM) / s)}


def reference(u_x, pos_x, Wq):
    y = mxq(f64(u_x), 2, "e5m2") @ mxq(f64(Wq), 1, "e5m2").T
    q = y.reshape(B, N, H, DH).transpose(0, 2, 1, 3)
    return rope_2d(q, f64(pos_x))

@@ -1,0 +1,206 @@
+import math
+from contextlib import ExitStack
+
+import concourse.mybir as mybir
+from concourse.masks import make_identity
+
+B, N_TOK, DIM, HEADS, DH = 2, 1024, 1024, 16, 64
+FLOPS = 2 * B * N_TOK * DIM * HEADS * DH
+
+F32 = mybir.dt.float32
+BF16 = mybir.dt.bfloat16
+I32 = mybir.dt.int32
+U32 = mybir.dt.uint32
+U8 = mybir.dt.uint8
+FP8X4 = mybir.dt.float8_e5m2_x4
+ALU = mybir.AluOpType
+ACT = mybir.ActivationFunctionType
+
+P = 128
+SLOTS = 4
+TURNS = [64.0 * 10000.0 ** (-j / 16.0) / (2.0 * math.pi) for j in range(16)]
+
+
+def tile_asymetrickernel_pb_kernel(tc, u_x, pos_x, Wq, out):
+    nc = tc.nc
+    with ExitStack() as ctx:
+        keep = ctx.enter_context(tc.tile_pool(name="keep", bufs=1))
+        stage = ctx.enter_context(tc.tile_pool(name="stage", bufs=3))
+        psum_t = ctx.enter_context(tc.psum_pool(name="psum_t", bufs=3))
+        psum_a = ctx.enter_context(tc.psum_pool(name="psum_a", bufs=5))
+
+        u_view = u_x.rearrange("b (c p t) k -> (b c) p t k", c=2, t=SLOTS)
+        pos_sb = keep.tile([P, 2, 2 * SLOTS], BF16, name="pos_sb")
+        nc.sync.dma_start(out=pos_sb[:], in_=pos_x.rearrange("o (c p t) d -> p (o c) (t d)", c=2, t=SLOTS))
+        w_words = []
+        u_words = []
+
+        def load_w(wt):
+            w_raw = keep.tile([P, DIM], BF16, name="w_raw%d" % wt)
+            nc.sync.dma_start(out=w_raw[:], in_=Wq[wt * P:(wt + 1) * P, :])
+            w_words.append(w_raw[:].bitcast(F32))
+
+        def load_u_slot(q, t):
+            u_raw = keep.tile([P, DIM], BF16, name="u_raw%d_%d" % (q, t))
+            nc.sync.dma_start(out=u_raw[:], in_=u_view[q, :, t, :])
+            u_words.append(u_raw[:].bitcast(F32))
+
+        def load_u_chunk(q):
+            u_raw = keep.tile([P, SLOTS, DIM], BF16, name="u_raw%d" % q)
+            nc.sync.dma_start(out=u_raw[:], in_=u_view[q])
+            for t in range(SLOTS):
+                u_words.append(u_raw[:, t, :].bitcast(F32))
+
+        load_w(0)
+        load_w(1)
+        load_u_slot(0, 0)
+        load_w(2)
+        load_w(3)
+        for t in range(1, SLOTS):
+            load_u_slot(0, t)
+        for wt in range(4, 8):
+            load_w(wt)
+        for q in range(1, 4):
+            load_u_chunk(q)
+
+        zero = keep.tile([P, 1], F32, name="zero")
+        nc.vector.memset(zero[:], 0.0)
+        warm = keep.tile([P, 1], F32, name="warm")
+        nc.scalar.activation(out=warm[:], in_=zero[:], func=ACT.Sin)
+
+        ident = keep.tile([P, P], F32, name="ident")
+        make_identity(nc, ident[:])
+        perm = keep.tile([P, P], F32, name="perm")
+        nc.gpsimd.tensor_copy(
+            out=perm[:].rearrange("p (a j s) -> p a j s", j=16, s=2),
+            in_=ident[:].rearrange("p (a s j) -> p a j s", s=2, j=16),
+        )
+
+        turns = keep.tile([P, 2, 16, 16], F32, name="turns")
+        for j in range(16):
+            nc.vector.tensor_scalar(
+                out=turns[:, 1, :, j], in0=pos_sb[:].rearrange("p c x -> p (c x)"),
+                scalar1=TURNS[j], scalar2=None, op0=ALU.mult,
+            )
+        nc.vector.tensor_scalar(out=turns[:, 0], in0=turns[:, 1], scalar1=0.25, scalar2=None, op0=ALU.add)
+        turns_flat = turns[:].rearrange("p w x j -> p (w x j)")
+        whole = keep.tile([P, 512], I32, name="whole")
+        nc.vector.tensor_copy(out=whole[:], in_=turns_flat)
+        frac = keep.tile([P, 512], F32, name="frac")
+        nc.vector.tensor_tensor(out=frac[:], in0=turns_flat, in1=whole[:], op=ALU.subtract)
+        negf = keep.tile([P, 2, 8, 32], F32, name="negf")
+        nc.vector.scalar_tensor_tensor(
+            out=negf[:].rearrange("p w s m -> p (w s m)"), in0=frac[:], scalar=0.5, in1=frac[:],
+            op0=ALU.is_gt, op1=ALU.subtract,
+        )
+        tab = keep.tile([P, 8, 4, 32], F32, name="tab")
+        two_pi = 2.0 * math.pi
+        for sd, which, scale in ((0, 0, -two_pi), (1, 1, -two_pi), (2, 1, two_pi), (3, 0, -two_pi)):
+            nc.scalar.activation(out=tab[:, :, sd, :], in_=negf[:, which], func=ACT.Sin, scale=scale)
+
+        u_codes = keep.tile([P, 16, 256], U32, name="u_codes", align_bytes=64)
+        u_scales = keep.tile([P, 16, 256], U8, name="u_scales", align_bytes=64)
+        w_codes = keep.tile([P, 2, 2, 512], U32, name="w_codes", align_bytes=64)
+        w_scales = keep.tile([P, 2, 2, 512], U8, name="w_scales", align_bytes=64)
+        w_grouped = []
+        for nh in range(2):
+            wg = keep.tile([P, 2, 512, 4], BF16, name="wg%d" % nh, align_bytes=64)
+            w_grouped.append(wg)
+
+        def transposes(words, mat):
+            xt = psum_t.tile([P, 2, 2, P], F32, name="xt")
+            for g in range(2):
+                for u in range(2):
+                    nc.tensor.transpose(xt[:, g, u, :], words[:, 256 * g + u:256 * (g + 1):2], mat[:])
+            return xt
+
+        def w_front(wt):
+            xt = transposes(w_words[wt], perm)
+            lo = (wt % 4) * P
+            nc.scalar.copy(
+                out=w_grouped[wt // 4][:].bitcast(F32)[:, :, lo:lo + P, :],
+                in_=xt[:].rearrange("p g u r -> p g r u"),
+            )
+
+        def w_quant(nh):
+            for g in range(2):
+                nc.vector.quantize_mx(
+                    out=w_codes[:, nh, g, :].bitcast(FP8X4), scales=w_scales[:, nh, g, :],
+                    in_=w_grouped[nh][:, g].rearrange("p n j -> p (n j)"),
+                )
+
+        def u_front(i):
+            xt = transposes(u_words[i], ident)
+            ug = stage.tile([P, 2, P, 4], BF16, name="ug", align_bytes=64)
+            nc.scalar.copy(out=ug[:].bitcast(F32), in_=xt[:].rearrange("p g u r -> p g r u"))
+            return ug
+
+        def u_quant(i, ug):
+            nc.vector.quantize_mx(
+                out=u_codes[:, i, :].bitcast(FP8X4), scales=u_scales[:, i, :],
+                in_=ug[:].rearrange("p g r j -> p (g r j)"),
+            )
+
+        def product(i, nh):
+            acc = psum_a.tile([P, 512], F32, name="acc")
+            for g in range(2):
+                cols = slice(g * P, (g + 1) * P)
+                nc.tensor.matmul_mx(
+                    out=acc[:],
+                    lhsT=u_codes[:, i, cols].bitcast(FP8X4), lhsT_scale=u_scales[:, i, cols],
+                    rhs=w_codes[:, nh, g, :].bitcast(FP8X4), rhs_scale=w_scales[:, nh, g, :],
+                    start=(g == 0), stop=(g == 1),
+                )
+            return acc
+
+        def rotate(acc, ts, res, t):
+            pr = stage.tile([P, 2, 2, 8, 32], F32, name="pr")
+            shape = [P, 2, 2, 8, 32]
+            nc.vector.tensor_tensor(
+                out=pr[:],
+                in0=acc[:].rearrange("p (h m s) -> p s h m", h=8, s=2).unsqueeze(2).to_broadcast(shape),
+                in1=tab[:, ts].rearrange("p (s e) m -> p s e m", s=2).unsqueeze(3).to_broadcast(shape),
+                op=ALU.mult,
+            )
+            nc.gpsimd.tensor_tensor(
+                out=res[:, :, t, :].rearrange("p h (d e j) -> p h d e j", d=2, e=2),
+                in0=pr[:, 0].rearrange("p e h (d j) -> p h d e j", d=2),
+                in1=pr[:, 1].rearrange("p e h (d j) -> p h d e j", d=2),
+                op=ALU.add,
+            )
+
+        w_front(0)
+        w_front(1)
+        pending = [(0, u_front(0))]
+        w_front(2)
+        w_front(3)
+        w_quant(0)
+        pending.append((1, u_front(1)))
+
+        fronts = {0: [("u", 2), ("w", 4)], 1: [("u", 3), ("w", 5)], 2: [("w", 6), ("w", 7)]}
+        for s in range(3, 15):
+            fronts[s] = [("u", s + 1)]
+
+        res = None
+        for s in range(32):
+            q, nh, t = s // 8, (s // 4) % 2, s % 4
+            for i, ug in pending:
+                u_quant(i, ug)
+            pending = []
+            if s == 3:
+                w_quant(1)
+            acc = product(4 * q + t, nh)
+            for kind, idx in fronts.get(s, []):
+                if kind == "u":
+                    pending.append((idx, u_front(idx)))
+                else:
+                    w_front(idx)
+            if t == 0:
+                res = stage.tile([P, 8, SLOTS, DH], F32, name="res")
+            rotate(acc, (q % 2) * SLOTS + t, res, t)
+            if t == SLOTS - 1:
+                b, c = q // 2, q % 2
+                nc.sync.dma_start(
+                    out=out[b, nh * 8:(nh + 1) * 8, c * 512:(c + 1) * 512, :].rearrange("h (p t) c -> p h (t c)", t=SLOTS),
+                    in_=res[:].rearrange("p h t c -> p h (t c)"),
+                )

@@ -45,12 +45,6 @@ def tile_asymetrickernel_pb_kernel(tc, u_x, pos_x, Wq, out):
             nc.sync.dma_start(out=u_raw[:], in_=u_view[q, :, t, :])
             u_words.append(u_raw[:].bitcast(F32))
 
-        def load_u_chunk(q):
-            u_raw = keep.tile([P, SLOTS, DIM], BF16, name="u_raw%d" % q)
-            nc.sync.dma_start(out=u_raw[:], in_=u_view[q])
-            for t in range(SLOTS):
-                u_words.append(u_raw[:, t, :].bitcast(F32))
-
         load_w(0)
         load_w(1)
         load_u_slot(0, 0)
@@ -61,7 +55,8 @@ def tile_asymetrickernel_pb_kernel(tc, u_x, pos_x, Wq, out):
         for wt in range(4, 8):
             load_w(wt)
         for q in range(1, 4):
-            load_u_chunk(q)
+            for t in range(SLOTS):
+                load_u_slot(q, t)
 
         zero = keep.tile([P, 1], F32, name="zero")
         nc.vector.memset(zero[:], 0.0)
@@ -95,8 +90,11 @@ def tile_asymetrickernel_pb_kernel(tc, u_x, pos_x, Wq, out):
         )
         tab = keep.tile([P, 8, 4, 32], F32, name="tab")
         two_pi = 2.0 * math.pi
-        for sd, which, scale in ((0, 0, -two_pi), (1, 1, -two_pi), (2, 1, two_pi), (3, 0, -two_pi)):
-            nc.scalar.activation(out=tab[:, :, sd, :], in_=negf[:, which], func=ACT.Sin, scale=scale)
+
+        def sines(c):
+            rows = slice(c * SLOTS, (c + 1) * SLOTS)
+            for sd, which, scale in ((0, 0, -two_pi), (1, 1, -two_pi), (2, 1, two_pi), (3, 0, -two_pi)):
+                nc.scalar.activation(out=tab[:, rows, sd, :], in_=negf[:, which, rows, :], func=ACT.Sin, scale=scale)
 
         u_codes = keep.tile([P, 16, 256], U32, name="u_codes", align_bytes=64)
         u_scales = keep.tile([P, 16, 256], U8, name="u_scales", align_bytes=64)
@@ -122,23 +120,29 @@ def tile_asymetrickernel_pb_kernel(tc, u_x, pos_x, Wq, out):
                 in_=xt[:].rearrange("p g u r -> p g r u"),
             )
 
-        def w_quant(nh):
-            for g in range(2):
-                nc.vector.quantize_mx(
-                    out=w_codes[:, nh, g, :].bitcast(FP8X4), scales=w_scales[:, nh, g, :],
-                    in_=w_grouped[nh][:, g].rearrange("p n j -> p (n j)"),
-                )
+        def w_quant(nh, g0, n):
+            nc.vector.quantize_mx(
+                out=w_codes[:, nh, g0:g0 + n, :].rearrange("p g n -> p (g n)").bitcast(FP8X4),
+                scales=w_scales[:, nh, g0:g0 + n, :].rearrange("p g n -> p (g n)"),
+                in_=w_grouped[nh][:, g0:g0 + n].rearrange("p g n j -> p (g n j)"),
+            )
+
+        u_grouped = {}
 
         def u_front(i):
+            q, t = divmod(i, SLOTS)
+            if t == 0:
+                ug = stage.tile([P, SLOTS, 2, P, 4], BF16, name="ug", align_bytes=64, bufs=2)
+                u_grouped[q] = ug
             xt = transposes(u_words[i], ident)
-            ug = stage.tile([P, 2, P, 4], BF16, name="ug", align_bytes=64)
-            nc.scalar.copy(out=ug[:].bitcast(F32), in_=xt[:].rearrange("p g u r -> p g r u"))
-            return ug
+            nc.scalar.copy(out=u_grouped[q][:, t].bitcast(F32), in_=xt[:].rearrange("p g u r -> p g r u"))
 
-        def u_quant(i, ug):
+        def u_quant(i, n):
+            q, t = divmod(i, SLOTS)
             nc.vector.quantize_mx(
-                out=u_codes[:, i, :].bitcast(FP8X4), scales=u_scales[:, i, :],
-                in_=ug[:].rearrange("p g r j -> p (g r j)"),
+                out=u_codes[:, i:i + n, :].rearrange("p i c -> p (i c)").bitcast(FP8X4),
+                scales=u_scales[:, i:i + n, :].rearrange("p i c -> p (i c)"),
+                in_=u_grouped[q][:, t:t + n].rearrange("p t g r j -> p (t g r j)"),
             )
 
         def product(i, nh):
@@ -171,36 +175,47 @@ def tile_asymetrickernel_pb_kernel(tc, u_x, pos_x, Wq, out):
 
         w_front(0)
         w_front(1)
-        pending = [(0, u_front(0))]
+        u_front(0)
         w_front(2)
         w_front(3)
-        w_quant(0)
-        pending.append((1, u_front(1)))
+        u_quant(0, 1)
+        w_quant(0, 0, 1)
+        w_quant(0, 1, 1)
+        sines(0)
+        u_front(1)
+        u_front(2)
+        u_front(3)
 
-        fronts = {0: [("u", 2), ("w", 4)], 1: [("u", 3), ("w", 5)], 2: [("w", 6), ("w", 7)]}
-        for s in range(3, 15):
-            fronts[s] = [("u", s + 1)]
+        fronts = {0: [("w", 4), ("w", 5)], 1: [("w", 6), ("w", 7)]}
+        for s in range(2, 14):
+            fronts[s] = [("u", s + 2)]
+        quants = {0: ("u", 1, 1), 1: ("u", 2, 2), 3: ("w", 1, 2), 6: ("u", 4, 4), 10: ("u", 8, 4), 14: ("u", 12, 4)}
 
         res = None
         for s in range(32):
             q, nh, t = s // 8, (s // 4) % 2, s % 4
-            for i, ug in pending:
-                u_quant(i, ug)
-            pending = []
-            if s == 3:
-                w_quant(1)
+            b, c = q // 2, q % 2
+            if s in quants:
+                kind, idx, n = quants[s]
+                if kind == "u":
+                    u_quant(idx, n)
+                else:
+                    w_quant(idx, 0, n)
             acc = product(4 * q + t, nh)
             for kind, idx in fronts.get(s, []):
                 if kind == "u":
-                    pending.append((idx, u_front(idx)))
+                    u_front(idx)
                 else:
                     w_front(idx)
+            if s == 2:
+                sines(1)
             if t == 0:
                 res = stage.tile([P, 8, SLOTS, DH], F32, name="res")
-            rotate(acc, (q % 2) * SLOTS + t, res, t)
-            if t == SLOTS - 1:
-                b, c = q // 2, q % 2
+            rotate(acc, c * SLOTS + t, res, t)
+            dst = out[b, nh * 8:(nh + 1) * 8, c * 512:(c + 1) * 512, :]
+            if s >= 28:
+                nc.sync.dma_start(out=dst.rearrange("h (p t) c -> p h t c", t=SLOTS)[:, :, t, :], in_=res[:, :, t, :])
+            elif t == SLOTS - 1:
                 nc.sync.dma_start(
-                    out=out[b, nh * 8:(nh + 1) * 8, c * 512:(c + 1) * 512, :].rearrange("h (p t) c -> p h (t c)", t=SLOTS),
-                    in_=res[:].rearrange("p h t c -> p h (t c)"),
+                    out=dst.rearrange("h (p t) c -> p h (t c)", t=SLOTS), in_=res[:].rearrange("p h t c -> p h (t c)"),
                 )

@@ -17,8 +17,12 @@ ALU = mybir.AluOpType
 ACT = mybir.ActivationFunctionType
 
 P = 128
+SPIN_FIRST = 5
+PAIR = 2
 SLOTS = 4
 TURNS = [64.0 * 10000.0 ** (-j / 16.0) / (2.0 * math.pi) for j in range(16)]
+SORT_LEAD, FRONT_LEAD, QUANT_LEAD = 6, 4, 2
+HEAD_TILES = (("u", 0), ("w", 0), ("w", 1), ("w", 2), ("w", 3))
 
 
 def tile_asymetrickernel_pb_kernel(tc, u_x, pos_x, Wq, out):
@@ -27,74 +31,84 @@ def tile_asymetrickernel_pb_kernel(tc, u_x, pos_x, Wq, out):
         keep = ctx.enter_context(tc.tile_pool(name="keep", bufs=1))
         stage = ctx.enter_context(tc.tile_pool(name="stage", bufs=3))
         psum_t = ctx.enter_context(tc.psum_pool(name="psum_t", bufs=3))
-        psum_a = ctx.enter_context(tc.psum_pool(name="psum_a", bufs=5))
+        psum_a = ctx.enter_context(tc.psum_pool(name="psum_a", bufs=4))
+        psum_w = ctx.enter_context(tc.psum_pool(name="psum_w", bufs=1))
+        ctx.enter_context(tc.manual_schedule())
 
-        u_view = u_x.rearrange("b (c p t) k -> (b c) p t k", c=2, t=SLOTS)
-        pos_sb = keep.tile([P, 2, 2 * SLOTS], BF16, name="pos_sb")
-        nc.sync.dma_start(out=pos_sb[:], in_=pos_x.rearrange("o (c p t) d -> p (o c) (t d)", c=2, t=SLOTS))
-        w_words = []
-        u_words = []
+        u_view = u_x.rearrange("b (p s) k -> b p s k", s=2 * SLOTS)
+        pos_sb = keep.tile([P, 4 * SLOTS], BF16, name="pos_sb")
+        nc.scalar.dma_start(out=pos_sb[:], in_=pos_x.rearrange("o (p s) d -> p (o s d)", s=2 * SLOTS))
+        w_words = {}
+        u_words = {}
 
-        def load_w(wt):
-            w_raw = keep.tile([P, DIM], BF16, name="w_raw%d" % wt)
-            nc.sync.dma_start(out=w_raw[:], in_=Wq[wt * P:(wt + 1) * P, :])
-            w_words.append(w_raw[:].bitcast(F32))
+        def load(kind, idx):
+            raw = keep.tile([P, DIM], BF16, name="raw_%s%d" % (kind, idx))
+            if kind == "w":
+                nc.sync.dma_start(out=raw[:], in_=Wq[idx * P:(idx + 1) * P, :])
+                w_words[idx] = raw[:].bitcast(F32)
+            else:
+                nc.sync.dma_start(out=raw[:], in_=u_view[idx // 8, :, idx % 8, :])
+                u_words[idx] = raw[:].bitcast(F32)
 
-        def load_u_slot(q, t):
-            u_raw = keep.tile([P, DIM], BF16, name="u_raw%d_%d" % (q, t))
-            nc.sync.dma_start(out=u_raw[:], in_=u_view[q, :, t, :])
-            u_words.append(u_raw[:].bitcast(F32))
+        for kind, idx in HEAD_TILES:
+            load(kind, idx)
+        for idx in range(1, 16):
+            load("u", idx)
+            if idx % 3 == 1 and idx < 12:
+                load("w", 4 + idx // 3)
 
-        load_w(0)
-        load_w(1)
-        load_u_slot(0, 0)
-        load_w(2)
-        load_w(3)
-        for t in range(1, SLOTS):
-            load_u_slot(0, t)
-        for wt in range(4, 8):
-            load_w(wt)
-        for q in range(1, 4):
-            for t in range(SLOTS):
-                load_u_slot(q, t)
-
-        zero = keep.tile([P, 1], F32, name="zero")
-        nc.vector.memset(zero[:], 0.0)
+        one = keep.tile([P, 1], F32, name="one")
+        nc.vector.memset(one[:], 1.0)
         warm = keep.tile([P, 1], F32, name="warm")
-        nc.scalar.activation(out=warm[:], in_=zero[:], func=ACT.Sin)
+        nc.scalar.activation(out=warm[:], in_=one[:], func=ACT.Sin)
+        idle_in = keep.tile([P, 512], BF16, name="idle_in")
+        nc.vector.memset(idle_in[:], 0.0)
+        idle_out = psum_w.tile([P, 512], F32, name="idle_out")
+        for k in range(SPIN_FIRST):
+            nc.tensor.matmul(out=idle_out[:], lhsT=idle_in[:, 0:P], rhs=idle_in[:], start=True, stop=True)
+        freq = keep.tile([P, 16], F32, name="freq")
+        for j in range(16):
+            nc.vector.tensor_scalar(out=freq[:, j:j + 1], in0=one[:], scalar1=TURNS[j], scalar2=None, op0=ALU.mult)
 
         ident = keep.tile([P, P], F32, name="ident")
         make_identity(nc, ident[:])
         perm = keep.tile([P, P], F32, name="perm")
         nc.gpsimd.tensor_copy(
-            out=perm[:].rearrange("p (a j s) -> p a j s", j=16, s=2),
-            in_=ident[:].rearrange("p (a s j) -> p a j s", s=2, j=16),
+            out=perm[:].rearrange("p (s a j) -> p s a j", s=2, j=16),
+            in_=ident[:].rearrange("p (a s j) -> p s a j", s=2, j=16),
         )
 
-        turns = keep.tile([P, 2, 16, 16], F32, name="turns")
-        for j in range(16):
-            nc.vector.tensor_scalar(
-                out=turns[:, 1, :, j], in0=pos_sb[:].rearrange("p c x -> p (c x)"),
-                scalar1=TURNS[j], scalar2=None, op0=ALU.mult,
-            )
-        nc.vector.tensor_scalar(out=turns[:, 0], in0=turns[:, 1], scalar1=0.25, scalar2=None, op0=ALU.add)
-        turns_flat = turns[:].rearrange("p w x j -> p (w x j)")
-        whole = keep.tile([P, 512], I32, name="whole")
-        nc.vector.tensor_copy(out=whole[:], in_=turns_flat)
-        frac = keep.tile([P, 512], F32, name="frac")
-        nc.vector.tensor_tensor(out=frac[:], in0=turns_flat, in1=whole[:], op=ALU.subtract)
+        turns = keep.tile([P, 2, 8, 32], F32, name="turns")
+        whole = keep.tile([P, 2, 8, 32], I32, name="whole")
+        frac = keep.tile([P, 2, 8, 32], F32, name="frac")
         negf = keep.tile([P, 2, 8, 32], F32, name="negf")
-        nc.vector.scalar_tensor_tensor(
-            out=negf[:].rearrange("p w s m -> p (w s m)"), in0=frac[:], scalar=0.5, in1=frac[:],
-            op0=ALU.is_gt, op1=ALU.subtract,
+        tab = keep.tile([P, 8, 2, DH], F32, name="tab")
+        nc.gpsimd.tensor_tensor(
+            out=turns[:, 1].rearrange("p s (d j) -> p (s d) j", d=2),
+            in0=pos_sb[:].unsqueeze(2).to_broadcast([P, 16, 16]),
+            in1=freq[:].unsqueeze(1).to_broadcast([P, 16, 16]),
+            op=ALU.mult,
         )
-        tab = keep.tile([P, 8, 4, 32], F32, name="tab")
+        nc.gpsimd.tensor_scalar(out=turns[:, 0], in0=turns[:, 1], scalar1=1.0, scalar2=0.25, op0=ALU.mult, op1=ALU.add)
+        nc.gpsimd.tensor_scalar(out=whole[:], in0=turns[:], scalar1=1.0, scalar2=0.0, op0=ALU.mult, op1=ALU.add)
         two_pi = 2.0 * math.pi
+
+        def fold(c):
+            rows = slice(c * SLOTS, (c + 1) * SLOTS)
+            nc.vector.tensor_tensor(out=frac[:, :, rows, :], in0=turns[:, :, rows, :], in1=whole[:, :, rows, :], op=ALU.subtract)
+            nc.vector.scalar_tensor_tensor(
+                out=negf[:, :, rows, :], in0=frac[:, :, rows, :], scalar=0.5, in1=frac[:, :, rows, :],
+                op0=ALU.is_gt, op1=ALU.subtract,
+            )
 
         def sines(c):
             rows = slice(c * SLOTS, (c + 1) * SLOTS)
-            for sd, which, scale in ((0, 0, -two_pi), (1, 1, -two_pi), (2, 1, two_pi), (3, 0, -two_pi)):
-                nc.scalar.activation(out=tab[:, rows, sd, :], in_=negf[:, which, rows, :], func=ACT.Sin, scale=scale)
+            for src, e, which, scale in ((0, 0, 0, -two_pi), (0, 1, 1, -two_pi), (1, 0, 1, two_pi), (1, 1, 0, -two_pi)):
+                nc.scalar.activation(
+                    out=tab[:, rows, src, :].rearrange("p s (d e j) -> p s d e j", d=2, e=2)[:, :, :, e, :],
+                    in_=negf[:, which, rows, :].rearrange("p s (d j) -> p s d j", d=2),
+                    func=ACT.Sin, scale=scale,
+                )
 
         u_codes = keep.tile([P, 16, 256], U32, name="u_codes", align_bytes=64)
         u_scales = keep.tile([P, 16, 256], U8, name="u_scales", align_bytes=64)
@@ -104,21 +118,43 @@ def tile_asymetrickernel_pb_kernel(tc, u_x, pos_x, Wq, out):
         for nh in range(2):
             wg = keep.tile([P, 2, 512, 4], BF16, name="wg%d" % nh, align_bytes=64)
             w_grouped.append(wg)
+        u_grouped = {}
 
-        def transposes(words, mat):
+        sorted_tiles = {}
+
+        def sort_words(kind, idx, on_vector):
+            words = w_words[idx] if kind == "w" else u_words[idx]
+            sorted_words = stage.tile([P, 2, 2, P], F32, name="sorted_words", bufs=4)
+            src = words.rearrange("p (g w u) -> p g u w", g=2, u=2)
+            if on_vector:
+                nc.vector.tensor_copy(out=sorted_words[:], in_=src)
+            else:
+                nc.scalar.copy(out=sorted_words[:], in_=src)
+            sorted_tiles[(kind, idx)] = sorted_words
+
+        def front(kind, idx):
+            words = w_words[idx] if kind == "w" else u_words[idx]
             xt = psum_t.tile([P, 2, 2, P], F32, name="xt")
+            mat = perm if kind == "w" else ident
             for g in range(2):
                 for u in range(2):
-                    nc.tensor.transpose(xt[:, g, u, :], words[:, 256 * g + u:256 * (g + 1):2], mat[:])
-            return xt
-
-        def w_front(wt):
-            xt = transposes(w_words[wt], perm)
-            lo = (wt % 4) * P
-            nc.scalar.copy(
-                out=w_grouped[wt // 4][:].bitcast(F32)[:, :, lo:lo + P, :],
-                in_=xt[:].rearrange("p g u r -> p g r u"),
-            )
+                    if (kind, idx) in sorted_tiles:
+                        nc.tensor.transpose(xt[:, g, u, :], sorted_tiles[(kind, idx)][:, g, u, :], mat[:])
+                    else:
+                        nc.tensor.transpose(xt[:, g, u, :], words[:, 256 * g + u:256 * (g + 1):2], mat[:])
+            if kind == "w":
+                lo = (idx % 4) * 64
+                for g in range(2):
+                    nc.scalar.copy(
+                        out=w_grouped[idx // 4][:].bitcast(F32)[:, g].rearrange("p (s n) u -> p s n u", s=2)[:, :, lo:lo + 64, :],
+                        in_=xt[:, g].rearrange("p u (s c) -> p s c u", s=2),
+                    )
+            else:
+                q, t = divmod(idx, SLOTS)
+                if t == 0:
+                    ug = stage.tile([P, SLOTS, 2, P, 4], BF16, name="ug", align_bytes=64, bufs=2)
+                    u_grouped[q] = ug
+                nc.scalar.copy(out=u_grouped[q][:, t].bitcast(F32), in_=xt[:].rearrange("p g u r -> p g r u"))
 
         def w_quant(nh, g0, n):
             nc.vector.quantize_mx(
@@ -126,16 +162,6 @@ def tile_asymetrickernel_pb_kernel(tc, u_x, pos_x, Wq, out):
                 scales=w_scales[:, nh, g0:g0 + n, :].rearrange("p g n -> p (g n)"),
                 in_=w_grouped[nh][:, g0:g0 + n].rearrange("p g n j -> p (g n j)"),
             )
-
-        u_grouped = {}
-
-        def u_front(i):
-            q, t = divmod(i, SLOTS)
-            if t == 0:
-                ug = stage.tile([P, SLOTS, 2, P, 4], BF16, name="ug", align_bytes=64, bufs=2)
-                u_grouped[q] = ug
-            xt = transposes(u_words[i], ident)
-            nc.scalar.copy(out=u_grouped[q][:, t].bitcast(F32), in_=xt[:].rearrange("p g u r -> p g r u"))
 
         def u_quant(i, n):
             q, t = divmod(i, SLOTS)
@@ -157,65 +183,81 @@ def tile_asymetrickernel_pb_kernel(tc, u_x, pos_x, Wq, out):
                 )
             return acc
 
-        def rotate(acc, ts, res, t):
-            pr = stage.tile([P, 2, 2, 8, 32], F32, name="pr")
-            shape = [P, 2, 2, 8, 32]
+        def multiply(acc, ts, pr_k):
+            shape = [P, 2, 8, 2, 2, 16]
             nc.vector.tensor_tensor(
-                out=pr[:],
-                in0=acc[:].rearrange("p (h m s) -> p s h m", h=8, s=2).unsqueeze(2).to_broadcast(shape),
-                in1=tab[:, ts].rearrange("p (s e) m -> p s e m", s=2).unsqueeze(3).to_broadcast(shape),
+                out=pr_k.rearrange("p s (h d e j) -> p s h d e j", h=8, d=2, e=2),
+                in0=acc[:].rearrange("p (s h d j) -> p s h d j", s=2, h=8, d=2).unsqueeze(4).to_broadcast(shape),
+                in1=tab[:, ts].rearrange("p s (d e j) -> p s d e j", d=2, e=2).unsqueeze(2).to_broadcast(shape),
                 op=ALU.mult,
             )
-            nc.gpsimd.tensor_tensor(
-                out=res[:, :, t, :].rearrange("p h (d e j) -> p h d e j", d=2, e=2),
-                in0=pr[:, 0].rearrange("p e h (d j) -> p h d e j", d=2),
-                in1=pr[:, 1].rearrange("p e h (d j) -> p h d e j", d=2),
+
+        def add(engine, pr, res, t0, n):
+            engine.tensor_tensor(
+                out=res[:, :, t0:t0 + n, :].rearrange("p h t c -> p t h c"),
+                in0=pr[:, 0:n, 0, :].rearrange("p k (h c) -> p k h c", h=8),
+                in1=pr[:, 0:n, 1, :].rearrange("p k (h c) -> p k h c", h=8),
                 op=ALU.add,
             )
 
-        w_front(0)
-        w_front(1)
-        u_front(0)
-        w_front(2)
-        w_front(3)
+        for kind, idx in HEAD_TILES:
+            sort_words(kind, idx, True)
+            front(kind, idx)
         u_quant(0, 1)
+        fold(0)
+        front("u", 1)
+        sines(0)
         w_quant(0, 0, 1)
         w_quant(0, 1, 1)
-        sines(0)
-        u_front(1)
-        u_front(2)
-        u_front(3)
+        u_quant(1, 1)
+        for n in range(2, FRONT_LEAD):
+            front("u", n)
+        for n in range(FRONT_LEAD, SORT_LEAD):
+            sort_words("u", n, False)
 
-        fronts = {0: [("w", 4), ("w", 5)], 1: [("w", 6), ("w", 7)]}
-        for s in range(2, 14):
-            fronts[s] = [("u", s + 2)]
-        quants = {0: ("u", 1, 1), 1: ("u", 2, 2), 3: ("w", 1, 2), 6: ("u", 4, 4), 10: ("u", 8, 4), 14: ("u", 12, 4)}
+        sorts = {}
+        fronts = {}
+        quants = {14: [("w", 1)]}
+        for n in range(2, 16):
+            if n >= SORT_LEAD:
+                sorts.setdefault(n - SORT_LEAD, []).append(("u", n))
+            if n >= FRONT_LEAD:
+                fronts.setdefault(n - FRONT_LEAD, []).append(("u", n))
+            quants.setdefault(n - QUANT_LEAD, []).append(("u", n))
+        for k in range(4):
+            sorts.setdefault(2 + 3 * k, []).append(("w", 4 + k))
+            fronts.setdefault(4 + 3 * k, []).append(("w", 4 + k))
 
         res = None
+        pr = None
         for s in range(32):
-            q, nh, t = s // 8, (s // 4) % 2, s % 4
+            nh, q, t = s // 16, (s // 4) % 4, s % 4
             b, c = q // 2, q % 2
-            if s in quants:
-                kind, idx, n = quants[s]
+            last_sweep = s >= 28
+            group = 1 if last_sweep else PAIR
+            for kind, idx in quants.get(s, []):
                 if kind == "u":
-                    u_quant(idx, n)
+                    u_quant(idx, 1)
                 else:
-                    w_quant(idx, 0, n)
+                    w_quant(idx, 0, 2)
+            if s == 1:
+                fold(1)
             acc = product(4 * q + t, nh)
             for kind, idx in fronts.get(s, []):
-                if kind == "u":
-                    u_front(idx)
-                else:
-                    w_front(idx)
+                front(kind, idx)
             if s == 2:
                 sines(1)
+            for kind, idx in sorts.get(s, []):
+                sort_words(kind, idx, False)
             if t == 0:
                 res = stage.tile([P, 8, SLOTS, DH], F32, name="res")
-            rotate(acc, c * SLOTS + t, res, t)
-            dst = out[b, nh * 8:(nh + 1) * 8, c * 512:(c + 1) * 512, :]
-            if s >= 28:
-                nc.sync.dma_start(out=dst.rearrange("h (p t) c -> p h t c", t=SLOTS)[:, :, t, :], in_=res[:, :, t, :])
+            if t % group == 0:
+                pr = stage.tile([P, PAIR, 2, 512], F32, name="pr")
+            multiply(acc, c * SLOTS + t, pr[:, t % group])
+            if t % group == group - 1:
+                add(nc.vector if s == 31 else nc.gpsimd, pr, res, t - group + 1, group)
+            dst = out[b, nh * 8:(nh + 1) * 8, :, :].rearrange("h (p s) c -> p h s c", s=2 * SLOTS)
+            if last_sweep:
+                nc.sync.dma_start(out=dst[:, :, c * SLOTS + t, :], in_=res[:, :, t, :])
             elif t == SLOTS - 1:
-                nc.sync.dma_start(
-                    out=dst.rearrange("h (p t) c -> p h (t c)", t=SLOTS), in_=res[:].rearrange("p h t c -> p h (t c)"),
-                )
+                nc.sync.dma_start(out=dst[:, :, c * SLOTS:(c + 1) * SLOTS, :], in_=res[:])

@@ -212,20 +212,15 @@ def tile_asymetrickernel_pb_kernel(tc, u_x, pos_x, Wq, out):
         u_quant(1, 1)
         for n in range(2, FRONT_LEAD):
             front("u", n)
-        for n in range(FRONT_LEAD, SORT_LEAD):
-            sort_words("u", n, False)
 
         sorts = {}
         fronts = {}
         quants = {14: [("w", 1)]}
         for n in range(2, 16):
-            if n >= SORT_LEAD:
-                sorts.setdefault(n - SORT_LEAD, []).append(("u", n))
             if n >= FRONT_LEAD:
                 fronts.setdefault(n - FRONT_LEAD, []).append(("u", n))
             quants.setdefault(n - QUANT_LEAD, []).append(("u", n))
         for k in range(4):
-            sorts.setdefault(2 + 3 * k, []).append(("w", 4 + k))
             fronts.setdefault(4 + 3 * k, []).append(("w", 4 + k))
 
         res = None

@@ -21,7 +21,7 @@ SPIN_FIRST = 5
 PAIR = 2
 SLOTS = 4
 TURNS = [64.0 * 10000.0 ** (-j / 16.0) / (2.0 * math.pi) for j in range(16)]
-SORT_LEAD, FRONT_LEAD, QUANT_LEAD = 6, 4, 2
+FRONT_LEAD, QUANT_LEAD = 4, 3
 HEAD_TILES = (("u", 0), ("w", 0), ("w", 1), ("w", 2), ("w", 3))
 
 
@@ -212,14 +212,15 @@ def tile_asymetrickernel_pb_kernel(tc, u_x, pos_x, Wq, out):
         u_quant(1, 1)
         for n in range(2, FRONT_LEAD):
             front("u", n)
+        u_quant(2, 1)
 
         sorts = {}
         fronts = {}
-        quants = {14: [("w", 1)]}
-        for n in range(2, 16):
-            if n >= FRONT_LEAD:
-                fronts.setdefault(n - FRONT_LEAD, []).append(("u", n))
-            quants.setdefault(n - QUANT_LEAD, []).append(("u", n))
+        quants = {0: [("u", 3, 1)], 13: [("w", 1, 2)]}
+        for n in range(4, 16):
+            fronts.setdefault(n - FRONT_LEAD, []).append(("u", n))
+            if n % 2 == 0:
+                quants.setdefault(n - QUANT_LEAD, []).append(("u", n, 2))
         for k in range(4):
             fronts.setdefault(4 + 3 * k, []).append(("w", 4 + k))
 
@@ -230,13 +231,6 @@ def tile_asymetrickernel_pb_kernel(tc, u_x, pos_x, Wq, out):
             b, c = q // 2, q % 2
             last_sweep = s >= 28
             group = 1 if last_sweep else PAIR
-            for kind, idx in quants.get(s, []):
-                if kind == "u":
-                    u_quant(idx, 1)
-                else:
-                    w_quant(idx, 0, 2)
-            if s == 1:
-                fold(1)
             acc = product(4 * q + t, nh)
             for kind, idx in fronts.get(s, []):
                 front(kind, idx)
@@ -249,6 +243,13 @@ def tile_asymetrickernel_pb_kernel(tc, u_x, pos_x, Wq, out):
             if t % group == 0:
                 pr = stage.tile([P, PAIR, 2, 512], F32, name="pr")
             multiply(acc, c * SLOTS + t, pr[:, t % group])
+            for kind, idx, n in quants.get(s, []):
+                if kind == "u":
+                    u_quant(idx, n)
+                else:
+                    w_quant(idx, 0, n)
+            if s == 0:
+                fold(1)
             if t % group == group - 1:
                 add(nc.vector if s == 31 else nc.gpsimd, pr, res, t - group + 1, group)
             dst = out[b, nh * 8:(nh + 1) * 8, :, :].rearrange("h (p s) c -> p h s c", s=2 * SLOTS)

@@ -210,13 +210,14 @@ def tile_asymetrickernel_pb_kernel(tc, u_x, pos_x, Wq, out):
         w_quant(0, 0, 1)
         w_quant(0, 1, 1)
         u_quant(1, 1)
+        fold(1)
         for n in range(2, FRONT_LEAD):
             front("u", n)
-        u_quant(2, 1)
+        u_quant(2, 2)
 
         sorts = {}
         fronts = {}
-        quants = {0: [("u", 3, 1)], 13: [("w", 1, 2)]}
+        quants = {13: [("w", 1, 2)]}
         for n in range(4, 16):
             fronts.setdefault(n - FRONT_LEAD, []).append(("u", n))
             if n % 2 == 0:
@@ -226,11 +227,12 @@ def tile_asymetrickernel_pb_kernel(tc, u_x, pos_x, Wq, out):
 
         res = None
         pr = None
+        owed = []
         for s in range(32):
             nh, q, t = s // 16, (s // 4) % 4, s % 4
             b, c = q // 2, q % 2
             last_sweep = s >= 28
-            group = 1 if last_sweep else PAIR
+            group = 1 if last_sweep or s < 2 else PAIR
             acc = product(4 * q + t, nh)
             for kind, idx in fronts.get(s, []):
                 front(kind, idx)
@@ -241,18 +243,23 @@ def tile_asymetrickernel_pb_kernel(tc, u_x, pos_x, Wq, out):
             if t == 0:
                 res = stage.tile([P, 8, SLOTS, DH], F32, name="res")
             if t % group == 0:
-                pr = stage.tile([P, PAIR, 2, 512], F32, name="pr")
+                pr = stage.tile([P, PAIR, 2, 512], F32, name="pr", bufs=4)
             multiply(acc, c * SLOTS + t, pr[:, t % group])
             for kind, idx, n in quants.get(s, []):
                 if kind == "u":
                     u_quant(idx, n)
                 else:
                     w_quant(idx, 0, n)
-            if s == 0:
-                fold(1)
-            if t % group == group - 1:
-                add(nc.vector if s == 31 else nc.gpsimd, pr, res, t - group + 1, group)
             dst = out[b, nh * 8:(nh + 1) * 8, :, :].rearrange("h (p s) c -> p h s c", s=2 * SLOTS)
+            if s > 28:
+                owed.append((pr, t))
+                if s == 31:
+                    for late_pr, late_t in owed:
+                        add(nc.vector, late_pr, res, late_t, 1)
+                        nc.sync.dma_start(out=dst[:, :, c * SLOTS + late_t, :], in_=res[:, :, late_t, :])
+                continue
+            if t % group == group - 1:
+                add(nc.gpsimd, pr, res, t - group + 1, group)
             if last_sweep:
                 nc.sync.dma_start(out=dst[:, :, c * SLOTS + t, :], in_=res[:, :, t, :])
             elif t == SLOTS - 1:

@@ -211,13 +211,13 @@ def tile_asymetrickernel_pb_kernel(tc, u_x, pos_x, Wq, out):
         w_quant(0, 1, 1)
         u_quant(1, 1)
         fold(1)
-        for n in range(2, FRONT_LEAD):
-            front("u", n)
-        u_quant(2, 2)
+        front("u", 2)
+        u_quant(2, 1)
 
         sorts = {}
         fronts = {}
-        quants = {13: [("w", 1, 2)]}
+        quants = {0: [("u", 3, 1)], 13: [("w", 1, 2)]}
+        fronts[0] = [("u", 3)]
         for n in range(4, 16):
             fronts.setdefault(n - FRONT_LEAD, []).append(("u", n))
             if n % 2 == 0:
@@ -227,12 +227,11 @@ def tile_asymetrickernel_pb_kernel(tc, u_x, pos_x, Wq, out):
 
         res = None
         pr = None
-        owed = []
         for s in range(32):
             nh, q, t = s // 16, (s // 4) % 4, s % 4
             b, c = q // 2, q % 2
             last_sweep = s >= 28
-            group = 1 if last_sweep or s < 2 else PAIR
+            group = 1 if s < 2 else PAIR
             acc = product(4 * q + t, nh)
             for kind, idx in fronts.get(s, []):
                 front(kind, idx)
@@ -251,16 +250,9 @@ def tile_asymetrickernel_pb_kernel(tc, u_x, pos_x, Wq, out):
                 else:
                     w_quant(idx, 0, n)
             dst = out[b, nh * 8:(nh + 1) * 8, :, :].rearrange("h (p s) c -> p h s c", s=2 * SLOTS)
-            if s > 28:
-                owed.append((pr, t))
-                if s == 31:
-                    for late_pr, late_t in owed:
-                        add(nc.vector, late_pr, res, late_t, 1)
-                        nc.sync.dma_start(out=dst[:, :, c * SLOTS + late_t, :], in_=res[:, :, late_t, :])
-                continue
             if t % group == group - 1:
-                add(nc.gpsimd, pr, res, t - group + 1, group)
-            if last_sweep:
-                nc.sync.dma_start(out=dst[:, :, c * SLOTS + t, :], in_=res[:, :, t, :])
+                add(nc.vector if s == 31 else nc.gpsimd, pr, res, t - group + 1, group)
+            if last_sweep and t % 2 == 1:
+                nc.sync.dma_start(out=dst[:, :, c * SLOTS + t - 1:c * SLOTS + t + 1, :], in_=res[:, :, t - 1:t + 1, :])
             elif t == SLOTS - 1:
                 nc.sync.dma_start(out=dst[:, :, c * SLOTS:(c + 1) * SLOTS, :], in_=res[:])

@@ -23,6 +23,9 @@ SLOTS = 4
 TURNS = [64.0 * 10000.0 ** (-j / 16.0) / (2.0 * math.pi) for j in range(16)]
 FRONT_LEAD, QUANT_LEAD = 4, 3
 HEAD_TILES = (("u", 0), ("w", 0), ("w", 1), ("w", 2), ("w", 3))
+SIDE_SLOTS = (0, 1)
+MAIN_TILES = (2, 3, 4, 5, 6, 7, 10, 11, 12, 13, 14, 15)
+SIDE_ADDS = {4: (0, 0), 5: (0, 1), 9: (1, 0), 11: (1, 1)}
 
 
 def tile_asymetrickernel_pb_kernel(tc, u_x, pos_x, Wq, out):
@@ -72,6 +75,8 @@ def tile_asymetrickernel_pb_kernel(tc, u_x, pos_x, Wq, out):
 
         ident = keep.tile([P, P], F32, name="ident")
         make_identity(nc, ident[:])
+        neg_ident = keep.tile([P, P], F32, name="neg_ident")
+        nc.gpsimd.tensor_scalar(out=neg_ident[:], in0=ident[:], scalar1=-1.0, scalar2=0.0, op0=ALU.mult, op1=ALU.add)
         perm = keep.tile([P, P], F32, name="perm")
         nc.gpsimd.tensor_copy(
             out=perm[:].rearrange("p (s a j) -> p s a j", s=2, j=16),
@@ -171,12 +176,17 @@ def tile_asymetrickernel_pb_kernel(tc, u_x, pos_x, Wq, out):
                 in_=u_grouped[q][:, t:t + n].rearrange("p t g r j -> p (t g r j)"),
             )
 
-        def product(i, nh):
-            acc = psum_a.tile([P, 512], F32, name="acc")
+        def product(i, nh, side=False):
+            if side:
+                bank = psum_t.tile([P, 2, 2, P], F32, name="xt")
+                acc = bank[:].rearrange("p a b c -> p (a b c)")
+            else:
+                bank = psum_a.tile([P, 512], F32, name="acc")
+                acc = bank[:]
             for g in range(2):
                 cols = slice(g * P, (g + 1) * P)
                 nc.tensor.matmul_mx(
-                    out=acc[:],
+                    out=acc,
                     lhsT=u_codes[:, i, cols].bitcast(FP8X4), lhsT_scale=u_scales[:, i, cols],
                     rhs=w_codes[:, nh, g, :].bitcast(FP8X4), rhs_scale=w_scales[:, nh, g, :],
                     start=(g == 0), stop=(g == 1),
@@ -187,7 +197,7 @@ def tile_asymetrickernel_pb_kernel(tc, u_x, pos_x, Wq, out):
             shape = [P, 2, 8, 2, 2, 16]
             nc.vector.tensor_tensor(
                 out=pr_k.rearrange("p s (h d e j) -> p s h d e j", h=8, d=2, e=2),
-                in0=acc[:].rearrange("p (s h d j) -> p s h d j", s=2, h=8, d=2).unsqueeze(4).to_broadcast(shape),
+                in0=acc.rearrange("p (s h d j) -> p s h d j", s=2, h=8, d=2).unsqueeze(4).to_broadcast(shape),
                 in1=tab[:, ts].rearrange("p s (d e j) -> p s d e j", d=2, e=2).unsqueeze(2).to_broadcast(shape),
                 op=ALU.mult,
             )
@@ -225,20 +235,68 @@ def tile_asymetrickernel_pb_kernel(tc, u_x, pos_x, Wq, out):
         for k in range(4):
             fronts.setdefault(4 + 3 * k, []).append(("w", 4 + k))
 
+        side_res = {}
+        side_prod = {}
+        side_y = {}
+
+        def side_gather(pair, accs):
+            y2 = stage.tile([P, 32, 2, 2, 8], F32, name="y2", bufs=1)
+            for b in range(2):
+                nc.scalar.copy(out=y2[:, :, :, b, :], in_=accs[b].rearrange("p (s h x) -> p x s h", s=2, h=8))
+            side_y[pair] = y2
+            prod = stage.tile([P, 2, 2, 2, 16, 16], F32, name="prod", bufs=2)
+            side_prod[pair] = prod
+
+        def side_rotate(pair, lo, hi):
+            y2, prod = side_y[pair], side_prod[pair]
+            for x in range(lo, hi):
+                d, j = divmod(x, 16)
+                for kind in range(2):
+                    col = 32 * d + 16 * kind + j
+                    nc.scalar.activation(
+                        out=prod[:, kind, :, d, j, :], in_=y2[:, x].rearrange("p s b h -> p s (b h)"),
+                        func=ACT.Copy, scale=tab[:, SIDE_SLOTS[pair], 0, col:col + 1],
+                    )
+
+        side_sums = {}
+
+        def side_add(pair, b):
+            prod = side_prod[pair]
+            bank = psum_t.tile([P, 2, 2, P], F32, name="xt")
+            heads = slice(8 * b, 8 * b + 8)
+            for e, terms in ((0, ((neg_ident, 1, 1), (ident, 0, 0))), (1, ((ident, 0, 1), (ident, 1, 0)))):
+                for n, (mat, kind, s) in enumerate(terms):
+                    nc.tensor.matmul(
+                        out=bank[:, e].rearrange("p d (j h) -> p d j h", h=8), lhsT=mat[:], rhs=prod[:, kind, s, :, :, heads],
+                        start=(n == 0), stop=(n == 1),
+                    )
+            side_sums[(pair, b)] = bank
+
+        def side_out(pair, b):
+            bank = side_sums[(pair, b)]
+            if pair == 0:
+                sr = stage.tile([P, 8, 2, DH], F32, name="side_res", bufs=2)
+                side_res[b] = sr
+            for e in range(2):
+                nc.scalar.copy(
+                    out=side_res[b][:, :, pair, :].rearrange("p h (d e j) -> p h d e j", d=2, e=2)[:, :, :, e, :],
+                    in_=bank[:, e].rearrange("p d (j h) -> p h d j", h=8),
+                )
+            if pair == 1:
+                dst = out[b, 8:16, :, :].rearrange("h (p s) c -> p h s c", s=2 * SLOTS)
+                nc.sync.dma_start(out=dst[:, :, 0:2, :], in_=side_res[b][:])
+
         res = None
         pr = None
-        for s in range(32):
-            nh, q, t = s // 16, (s // 4) % 4, s % 4
+        for s in range(16):
+            q, t = divmod(s, 4)
             b, c = q // 2, q % 2
-            last_sweep = s >= 28
             group = 1 if s < 2 else PAIR
-            acc = product(4 * q + t, nh)
+            acc = product(s, 0)
             for kind, idx in fronts.get(s, []):
                 front(kind, idx)
             if s == 2:
                 sines(1)
-            for kind, idx in sorts.get(s, []):
-                sort_words(kind, idx, False)
             if t == 0:
                 res = stage.tile([P, 8, SLOTS, DH], F32, name="res")
             if t % group == 0:
@@ -249,10 +307,44 @@ def tile_asymetrickernel_pb_kernel(tc, u_x, pos_x, Wq, out):
                     u_quant(idx, n)
                 else:
                     w_quant(idx, 0, n)
-            dst = out[b, nh * 8:(nh + 1) * 8, :, :].rearrange("h (p s) c -> p h s c", s=2 * SLOTS)
+            dst = out[b, 0:8, :, :].rearrange("h (p s) c -> p h s c", s=2 * SLOTS)
             if t % group == group - 1:
-                add(nc.vector if s == 31 else nc.gpsimd, pr, res, t - group + 1, group)
-            if last_sweep and t % 2 == 1:
+                add(nc.gpsimd, pr, res, t - group + 1, group)
+            if t == SLOTS - 1:
+                nc.sync.dma_start(out=dst[:, :, c * SLOTS:(c + 1) * SLOTS, :], in_=res[:])
+
+        side_accs = [[product(8 * b + slot, 1, True) for b in range(2)] for slot in SIDE_SLOTS[0:1]]
+        side_gather(0, side_accs[0])
+        side_rotate(0, 0, 32)
+        for k, i in enumerate(MAIN_TILES):
+            q, t = divmod(i, 4)
+            b, c = q // 2, q % 2
+            last = k == len(MAIN_TILES) - 1
+            acc = product(i, 1)
+            if k == 1:
+                accs = [product(8 * bb + SIDE_SLOTS[1], 1, True) for bb in range(2)]
+                side_gather(1, accs)
+                side_rotate(1, 0, 16)
+            if k in SIDE_ADDS:
+                side_add(SIDE_ADDS[k][0], SIDE_ADDS[k][1])
+            if k == 4:
+                side_out(0, 0)
+                side_rotate(1, 16, 32)
+            if k == 5:
+                side_out(0, 1)
+            if k == 9:
+                side_out(1, 0)
+            if k == 11:
+                side_out(1, 1)
+            if t == 0 or k == 0 or i == 10:
+                res = stage.tile([P, 8, SLOTS, DH], F32, name="res")
+            if t % 2 == 0:
+                pr = stage.tile([P, PAIR, 2, 512], F32, name="pr", bufs=4)
+            multiply(acc, c * SLOTS + t, pr[:, t % 2])
+            dst = out[b, 8:16, :, :].rearrange("h (p s) c -> p h s c", s=2 * SLOTS)
+            if t % 2 == 1:
+                add(nc.vector if last else nc.gpsimd, pr, res, t - 1, 2)
+            if (c == 0 or q == 3) and t % 2 == 1:
                 nc.sync.dma_start(out=dst[:, :, c * SLOTS + t - 1:c * SLOTS + t + 1, :], in_=res[:, :, t - 1:t + 1, :])
             elif t == SLOTS - 1:
                 nc.sync.dma_start(out=dst[:, :, c * SLOTS:(c + 1) * SLOTS, :], in_=res[:])

@@ -23,9 +23,9 @@ SLOTS = 4
 TURNS = [64.0 * 10000.0 ** (-j / 16.0) / (2.0 * math.pi) for j in range(16)]
 FRONT_LEAD, QUANT_LEAD = 4, 3
 HEAD_TILES = (("u", 0), ("w", 0), ("w", 1), ("w", 2), ("w", 3))
-SIDE_SLOTS = (0, 1)
-MAIN_TILES = (2, 3, 4, 5, 6, 7, 10, 11, 12, 13, 14, 15)
-SIDE_ADDS = {4: (0, 0), 5: (0, 1), 9: (1, 0), 11: (1, 1)}
+SIDE_SLOT = 0
+MAIN_GROUPS = ((1,), (2, 3), (4, 5), (6, 7), (9,), (10, 11), (12, 13), (14, 15))
+SIDE_ADDS = {6: (0, 0), 7: (0, 1), 8: (1, 0), 9: (1, 1)}
 
 
 def tile_asymetrickernel_pb_kernel(tc, u_x, pos_x, Wq, out):
@@ -75,8 +75,6 @@ def tile_asymetrickernel_pb_kernel(tc, u_x, pos_x, Wq, out):
 
         ident = keep.tile([P, P], F32, name="ident")
         make_identity(nc, ident[:])
-        neg_ident = keep.tile([P, P], F32, name="neg_ident")
-        nc.gpsimd.tensor_scalar(out=neg_ident[:], in0=ident[:], scalar1=-1.0, scalar2=0.0, op0=ALU.mult, op1=ALU.add)
         perm = keep.tile([P, P], F32, name="perm")
         nc.gpsimd.tensor_copy(
             out=perm[:].rearrange("p (s a j) -> p s a j", s=2, j=16),
@@ -96,6 +94,8 @@ def tile_asymetrickernel_pb_kernel(tc, u_x, pos_x, Wq, out):
         )
         nc.gpsimd.tensor_scalar(out=turns[:, 0], in0=turns[:, 1], scalar1=1.0, scalar2=0.25, op0=ALU.mult, op1=ALU.add)
         nc.gpsimd.tensor_scalar(out=whole[:], in0=turns[:], scalar1=1.0, scalar2=0.0, op0=ALU.mult, op1=ALU.add)
+        neg_ident = keep.tile([P, P], F32, name="neg_ident")
+        nc.gpsimd.tensor_scalar(out=neg_ident[:], in0=ident[:], scalar1=-1.0, scalar2=0.0, op0=ALU.mult, op1=ALU.add)
         two_pi = 2.0 * math.pi
 
         def fold(c):
@@ -235,56 +235,45 @@ def tile_asymetrickernel_pb_kernel(tc, u_x, pos_x, Wq, out):
         for k in range(4):
             fronts.setdefault(4 + 3 * k, []).append(("w", 4 + k))
 
-        side_res = {}
-        side_prod = {}
-        side_y = {}
+        y2 = stage.tile([P, 32, 2, 2, 8], F32, name="y2", bufs=1)
+        prod = stage.tile([P, 2, 2, 2, 16, 16], F32, name="prod", bufs=1)
 
-        def side_gather(pair, accs):
-            y2 = stage.tile([P, 32, 2, 2, 8], F32, name="y2", bufs=1)
+        def side_gather(accs):
             for b in range(2):
                 nc.scalar.copy(out=y2[:, :, :, b, :], in_=accs[b].rearrange("p (s h x) -> p x s h", s=2, h=8))
-            side_y[pair] = y2
-            prod = stage.tile([P, 2, 2, 2, 16, 16], F32, name="prod", bufs=2)
-            side_prod[pair] = prod
 
-        def side_rotate(pair, lo, hi):
-            y2, prod = side_y[pair], side_prod[pair]
+        def side_rotate(lo, hi):
             for x in range(lo, hi):
                 d, j = divmod(x, 16)
                 for kind in range(2):
                     col = 32 * d + 16 * kind + j
                     nc.scalar.activation(
                         out=prod[:, kind, :, d, j, :], in_=y2[:, x].rearrange("p s b h -> p s (b h)"),
-                        func=ACT.Copy, scale=tab[:, SIDE_SLOTS[pair], 0, col:col + 1],
+                        func=ACT.Copy, scale=tab[:, SIDE_SLOT, 0, col:col + 1],
                     )
 
-        side_sums = {}
+        side_tiles = {}
 
-        def side_add(pair, b):
-            prod = side_prod[pair]
-            bank = psum_t.tile([P, 2, 2, P], F32, name="xt")
+        def side_finish(b, e):
+            if e == 0:
+                bank = psum_t.tile([P, 2, 2, P], F32, name="xt")
+                side_res = stage.tile([P, 8, DH], F32, name="side_res", bufs=2)
+                side_tiles[b] = (bank, side_res)
+            bank, side_res = side_tiles[b]
             heads = slice(8 * b, 8 * b + 8)
-            for e, terms in ((0, ((neg_ident, 1, 1), (ident, 0, 0))), (1, ((ident, 0, 1), (ident, 1, 0)))):
-                for n, (mat, kind, s) in enumerate(terms):
-                    nc.tensor.matmul(
-                        out=bank[:, e].rearrange("p d (j h) -> p d j h", h=8), lhsT=mat[:], rhs=prod[:, kind, s, :, :, heads],
-                        start=(n == 0), stop=(n == 1),
-                    )
-            side_sums[(pair, b)] = bank
-
-        def side_out(pair, b):
-            bank = side_sums[(pair, b)]
-            if pair == 0:
-                sr = stage.tile([P, 8, 2, DH], F32, name="side_res", bufs=2)
-                side_res[b] = sr
-            for e in range(2):
-                nc.scalar.copy(
-                    out=side_res[b][:, :, pair, :].rearrange("p h (d e j) -> p h d e j", d=2, e=2)[:, :, :, e, :],
-                    in_=bank[:, e].rearrange("p d (j h) -> p h d j", h=8),
+            terms = ((neg_ident, 1, 1), (ident, 0, 0)) if e == 0 else ((ident, 0, 1), (ident, 1, 0))
+            for n, (mat, kind, s) in enumerate(terms):
+                nc.tensor.matmul(
+                    out=bank[:, e].rearrange("p d (j h) -> p d j h", h=8), lhsT=mat[:], rhs=prod[:, kind, s, :, :, heads],
+                    start=(n == 0), stop=(n == 1),
                 )
-            if pair == 1:
+            nc.scalar.copy(
+                out=side_res[:].rearrange("p h (d e j) -> p h d e j", d=2, e=2)[:, :, :, e, :],
+                in_=bank[:, e].rearrange("p d (j h) -> p h d j", h=8),
+            )
+            if e == 1:
                 dst = out[b, 8:16, :, :].rearrange("h (p s) c -> p h s c", s=2 * SLOTS)
-                nc.sync.dma_start(out=dst[:, :, 0:2, :], in_=side_res[b][:])
+                nc.sync.dma_start(out=dst[:, :, SIDE_SLOT, :], in_=side_res[:])
 
         res = None
         pr = None
@@ -313,38 +302,26 @@ def tile_asymetrickernel_pb_kernel(tc, u_x, pos_x, Wq, out):
             if t == SLOTS - 1:
                 nc.sync.dma_start(out=dst[:, :, c * SLOTS:(c + 1) * SLOTS, :], in_=res[:])
 
-        side_accs = [[product(8 * b + slot, 1, True) for b in range(2)] for slot in SIDE_SLOTS[0:1]]
-        side_gather(0, side_accs[0])
-        side_rotate(0, 0, 32)
-        for k, i in enumerate(MAIN_TILES):
-            q, t = divmod(i, 4)
+        side_gather([product(8 * b + SIDE_SLOT, 1, True) for b in range(2)])
+        side_rotate(0, 32)
+        k = 0
+        for tiles in MAIN_GROUPS:
+            n = len(tiles)
+            pr = stage.tile([P, PAIR, 2, 512], F32, name="pr", bufs=4)
+            q, t0 = divmod(tiles[0], 4)
             b, c = q // 2, q % 2
-            last = k == len(MAIN_TILES) - 1
-            acc = product(i, 1)
-            if k == 1:
-                accs = [product(8 * bb + SIDE_SLOTS[1], 1, True) for bb in range(2)]
-                side_gather(1, accs)
-                side_rotate(1, 0, 16)
-            if k in SIDE_ADDS:
-                side_add(SIDE_ADDS[k][0], SIDE_ADDS[k][1])
-            if k == 4:
-                side_out(0, 0)
-                side_rotate(1, 16, 32)
-            if k == 5:
-                side_out(0, 1)
-            if k == 9:
-                side_out(1, 0)
-            if k == 11:
-                side_out(1, 1)
-            if t == 0 or k == 0 or i == 10:
+            if t0 == 0 or n == 1:
                 res = stage.tile([P, 8, SLOTS, DH], F32, name="res")
-            if t % 2 == 0:
-                pr = stage.tile([P, PAIR, 2, 512], F32, name="pr", bufs=4)
-            multiply(acc, c * SLOTS + t, pr[:, t % 2])
+            for m, i in enumerate(tiles):
+                acc = product(i, 1)
+                if k in SIDE_ADDS:
+                    side_finish(SIDE_ADDS[k][0], SIDE_ADDS[k][1])
+                multiply(acc, i % 8, pr[:, m])
+                k += 1
+            add(nc.vector if tiles[-1] == 15 else nc.gpsimd, pr, res, t0, n)
             dst = out[b, 8:16, :, :].rearrange("h (p s) c -> p h s c", s=2 * SLOTS)
-            if t % 2 == 1:
-                add(nc.vector if last else nc.gpsimd, pr, res, t - 1, 2)
-            if (c == 0 or q == 3) and t % 2 == 1:
-                nc.sync.dma_start(out=dst[:, :, c * SLOTS + t - 1:c * SLOTS + t + 1, :], in_=res[:, :, t - 1:t + 1, :])
-            elif t == SLOTS - 1:
-                nc.sync.dma_start(out=dst[:, :, c * SLOTS:(c + 1) * SLOTS, :], in_=res[:])
+            if q == 3:
+                nc.sync.dma_start(out=dst[:, :, c * SLOTS + t0:c * SLOTS + t0 + 2, :], in_=res[:, :, t0:t0 + 2, :])
+            elif t0 == 2:
+                lo = 1 if c == 0 else 0
+                nc.sync.dma_start(out=dst[:, :, c * SLOTS + lo:(c + 1) * SLOTS, :], in_=res[:, :, lo:SLOTS, :])

@@ -24,7 +24,7 @@ TURNS = [64.0 * 10000.0 ** (-j / 16.0) / (2.0 * math.pi) for j in range(16)]
 FRONT_LEAD, QUANT_LEAD = 4, 3
 HEAD_TILES = (("u", 0), ("w", 0), ("w", 1), ("w", 2), ("w", 3))
 SIDE_SLOT = 0
-MAIN_GROUPS = ((1,), (2, 3), (4, 5), (6, 7), (9,), (10, 11), (12, 13), (14, 15))
+MAIN_GROUPS = ((1, 9), (2, 3), (4, 5), (6, 7), (10, 11), (12, 13), (14, 15))
 SIDE_ADDS = {6: (0, 0), 7: (0, 1), 8: (1, 0), 9: (1, 1)}
 
 
@@ -252,28 +252,24 @@ def tile_asymetrickernel_pb_kernel(tc, u_x, pos_x, Wq, out):
                         func=ACT.Copy, scale=tab[:, SIDE_SLOT, 0, col:col + 1],
                     )
 
-        side_tiles = {}
+        low_res = stage.tile([P, 2, 8, 2, DH], F32, name="low_res", bufs=1)
 
         def side_finish(b, e):
-            if e == 0:
-                bank = psum_t.tile([P, 2, 2, P], F32, name="xt")
-                side_res = stage.tile([P, 8, DH], F32, name="side_res", bufs=2)
-                side_tiles[b] = (bank, side_res)
-            bank, side_res = side_tiles[b]
+            bank = psum_t.tile([P, 2, 2, P], F32, name="xt")
             heads = slice(8 * b, 8 * b + 8)
             terms = ((neg_ident, 1, 1), (ident, 0, 0)) if e == 0 else ((ident, 0, 1), (ident, 1, 0))
             for n, (mat, kind, s) in enumerate(terms):
                 nc.tensor.matmul(
-                    out=bank[:, e].rearrange("p d (j h) -> p d j h", h=8), lhsT=mat[:], rhs=prod[:, kind, s, :, :, heads],
+                    out=bank[:, 0].rearrange("p d (j h) -> p d j h", h=8), lhsT=mat[:], rhs=prod[:, kind, s, :, :, heads],
                     start=(n == 0), stop=(n == 1),
                 )
             nc.scalar.copy(
-                out=side_res[:].rearrange("p h (d e j) -> p h d e j", d=2, e=2)[:, :, :, e, :],
-                in_=bank[:, e].rearrange("p d (j h) -> p h d j", h=8),
+                out=low_res[:, b, :, SIDE_SLOT, :].rearrange("p h (d e j) -> p h d e j", d=2, e=2)[:, :, :, e, :],
+                in_=bank[:, 0].rearrange("p d (j h) -> p h d j", h=8),
             )
             if e == 1:
                 dst = out[b, 8:16, :, :].rearrange("h (p s) c -> p h s c", s=2 * SLOTS)
-                nc.sync.dma_start(out=dst[:, :, SIDE_SLOT, :], in_=side_res[:])
+                nc.sync.dma_start(out=dst[:, :, 0:2, :], in_=low_res[:, b])
 
         res = None
         pr = None
@@ -306,11 +302,10 @@ def tile_asymetrickernel_pb_kernel(tc, u_x, pos_x, Wq, out):
         side_rotate(0, 32)
         k = 0
         for tiles in MAIN_GROUPS:
-            n = len(tiles)
             pr = stage.tile([P, PAIR, 2, 512], F32, name="pr", bufs=4)
             q, t0 = divmod(tiles[0], 4)
             b, c = q // 2, q % 2
-            if t0 == 0 or n == 1:
+            if t0 == 0 or (c == 0 and t0 == 2):
                 res = stage.tile([P, 8, SLOTS, DH], F32, name="res")
             for m, i in enumerate(tiles):
                 acc = product(i, 1)
@@ -318,10 +313,17 @@ def tile_asymetrickernel_pb_kernel(tc, u_x, pos_x, Wq, out):
                     side_finish(SIDE_ADDS[k][0], SIDE_ADDS[k][1])
                 multiply(acc, i % 8, pr[:, m])
                 k += 1
-            add(nc.vector if tiles[-1] == 15 else nc.gpsimd, pr, res, t0, n)
+            if t0 == 1:
+                nc.gpsimd.tensor_tensor(
+                    out=low_res[:, :, :, 1, :],
+                    in0=pr[:, :, 0, :].rearrange("p k (h c) -> p k h c", h=8),
+                    in1=pr[:, :, 1, :].rearrange("p k (h c) -> p k h c", h=8),
+                    op=ALU.add,
+                )
+                continue
+            add(nc.vector if tiles[-1] == 15 else nc.gpsimd, pr, res, t0, 2)
             dst = out[b, 8:16, :, :].rearrange("h (p s) c -> p h s c", s=2 * SLOTS)
-            if q == 3:
+            if c == 0 or q == 3:
                 nc.sync.dma_start(out=dst[:, :, c * SLOTS + t0:c * SLOTS + t0 + 2, :], in_=res[:, :, t0:t0 + 2, :])
             elif t0 == 2:
-                lo = 1 if c == 0 else 0
-                nc.sync.dma_start(out=dst[:, :, c * SLOTS + lo:(c + 1) * SLOTS, :], in_=res[:, :, lo:SLOTS, :])
+                nc.sync.dma_start(out=dst[:, :, c * SLOTS:(c + 1) * SLOTS, :], in_=res[:])

@@ -202,11 +202,11 @@ def tile_asymetrickernel_pb_kernel(tc, u_x, pos_x, Wq, out):
                 op=ALU.mult,
             )
 
-        def add(engine, pr, res, t0, n):
+        def add(engine, pr, res, t0, n, heads=slice(0, 8)):
             engine.tensor_tensor(
-                out=res[:, :, t0:t0 + n, :].rearrange("p h t c -> p t h c"),
-                in0=pr[:, 0:n, 0, :].rearrange("p k (h c) -> p k h c", h=8),
-                in1=pr[:, 0:n, 1, :].rearrange("p k (h c) -> p k h c", h=8),
+                out=res[:, heads, t0:t0 + n, :].rearrange("p h t c -> p t h c"),
+                in0=pr[:, 0:n, 0, :].rearrange("p k (h c) -> p k h c", h=8)[:, :, heads, :],
+                in1=pr[:, 0:n, 1, :].rearrange("p k (h c) -> p k h c", h=8)[:, :, heads, :],
                 op=ALU.add,
             )
 
@@ -321,9 +321,14 @@ def tile_asymetrickernel_pb_kernel(tc, u_x, pos_x, Wq, out):
                     op=ALU.add,
                 )
                 continue
-            add(nc.vector if tiles[-1] == 15 else nc.gpsimd, pr, res, t0, 2)
             dst = out[b, 8:16, :, :].rearrange("h (p s) c -> p h s c", s=2 * SLOTS)
-            if c == 0 or q == 3:
+            if q == 3:
+                for heads in (slice(0, 4), slice(4, 8)):
+                    add(nc.vector if tiles[-1] == 15 else nc.gpsimd, pr, res, t0, 2, heads)
+                    nc.sync.dma_start(out=dst[:, heads, c * SLOTS + t0:c * SLOTS + t0 + 2, :], in_=res[:, heads, t0:t0 + 2, :])
+                continue
+            add(nc.gpsimd, pr, res, t0, 2)
+            if c == 0:
                 nc.sync.dma_start(out=dst[:, :, c * SLOTS + t0:c * SLOTS + t0 + 2, :], in_=res[:, :, t0:t0 + 2, :])
             elif t0 == 2:
                 nc.sync.dma_start(out=dst[:, :, c * SLOTS:(c + 1) * SLOTS, :], in_=res[:])

import math
from contextlib import ExitStack

import concourse.mybir as mybir
from concourse.masks import make_identity

B, N_TOK, DIM, HEADS, DH = 2, 1024, 1024, 16, 64
FLOPS = 2 * B * N_TOK * DIM * HEADS * DH

F32 = mybir.dt.float32
BF16 = mybir.dt.bfloat16
I32 = mybir.dt.int32
U32 = mybir.dt.uint32
U8 = mybir.dt.uint8
FP8X4 = mybir.dt.float8_e5m2_x4
ALU = mybir.AluOpType
ACT = mybir.ActivationFunctionType

P = 128
SPIN_FIRST = 5
PAIR = 2
SLOTS = 4
TURNS = [64.0 * 10000.0 ** (-j / 16.0) / (2.0 * math.pi) for j in range(16)]
FRONT_LEAD, QUANT_LEAD = 4, 3
HEAD_TILES = (("u", 0), ("w", 0), ("w", 1), ("w", 2), ("w", 3))
SIDE_SLOT = 0
MAIN_GROUPS = ((1, 9), (2, 3), (4, 5), (6, 7), (10, 11), (12, 13), (14, 15))
SIDE_ADDS = {6: (0, 0), 7: (0, 1), 8: (1, 0), 9: (1, 1)}


def tile_asymetrickernel_pb_kernel(tc, u_x, pos_x, Wq, out):
    nc = tc.nc
    with ExitStack() as ctx:
        keep = ctx.enter_context(tc.tile_pool(name="keep", bufs=1))
        stage = ctx.enter_context(tc.tile_pool(name="stage", bufs=3))
        psum_t = ctx.enter_context(tc.psum_pool(name="psum_t", bufs=3))
        psum_a = ctx.enter_context(tc.psum_pool(name="psum_a", bufs=4))
        psum_w = ctx.enter_context(tc.psum_pool(name="psum_w", bufs=1))
        ctx.enter_context(tc.manual_schedule())

        u_view = u_x.rearrange("b (p s) k -> b p s k", s=2 * SLOTS)
        pos_sb = keep.tile([P, 4 * SLOTS], BF16, name="pos_sb")
        nc.scalar.dma_start(out=pos_sb[:], in_=pos_x.rearrange("o (p s) d -> p (o s d)", s=2 * SLOTS))
        w_words = {}
        u_words = {}

        def load(kind, idx):
            raw = keep.tile([P, DIM], BF16, name="raw_%s%d" % (kind, idx))
            if kind == "w":
                nc.sync.dma_start(out=raw[:], in_=Wq[idx * P:(idx + 1) * P, :])
                w_words[idx] = raw[:].bitcast(F32)
            else:
                nc.sync.dma_start(out=raw[:], in_=u_view[idx // 8, :, idx % 8, :])
                u_words[idx] = raw[:].bitcast(F32)

        for kind, idx in HEAD_TILES:
            load(kind, idx)
        for idx in range(1, 16):
            load("u", idx)
            if idx % 3 == 1 and idx < 12:
                load("w", 4 + idx // 3)

        one = keep.tile([P, 1], F32, name="one")
        nc.vector.memset(one[:], 1.0)
        warm = keep.tile([P, 1], F32, name="warm")
        nc.scalar.activation(out=warm[:], in_=one[:], func=ACT.Sin)
        idle_in = keep.tile([P, 512], BF16, name="idle_in")
        nc.vector.memset(idle_in[:], 0.0)
        idle_out = psum_w.tile([P, 512], F32, name="idle_out")
        for k in range(SPIN_FIRST):
            nc.tensor.matmul(out=idle_out[:], lhsT=idle_in[:, 0:P], rhs=idle_in[:], start=True, stop=True)
        freq = keep.tile([P, 16], F32, name="freq")
        for j in range(16):
            nc.vector.tensor_scalar(out=freq[:, j:j + 1], in0=one[:], scalar1=TURNS[j], scalar2=None, op0=ALU.mult)

        ident = keep.tile([P, P], F32, name="ident")
        make_identity(nc, ident[:])
        perm = keep.tile([P, P], F32, name="perm")
        nc.gpsimd.tensor_copy(
            out=perm[:].rearrange("p (s a j) -> p s a j", s=2, j=16),
            in_=ident[:].rearrange("p (a s j) -> p s a j", s=2, j=16),
        )

        turns = keep.tile([P, 2, 8, 32], F32, name="turns")
        whole = keep.tile([P, 2, 8, 32], I32, name="whole")
        frac = keep.tile([P, 2, 8, 32], F32, name="frac")
        negf = keep.tile([P, 2, 8, 32], F32, name="negf")
        tab = keep.tile([P, 8, 2, DH], F32, name="tab")
        nc.gpsimd.tensor_tensor(
            out=turns[:, 1].rearrange("p s (d j) -> p (s d) j", d=2),
            in0=pos_sb[:].unsqueeze(2).to_broadcast([P, 16, 16]),
            in1=freq[:].unsqueeze(1).to_broadcast([P, 16, 16]),
            op=ALU.mult,
        )
        nc.gpsimd.tensor_scalar(out=turns[:, 0], in0=turns[:, 1], scalar1=1.0, scalar2=0.25, op0=ALU.mult, op1=ALU.add)
        nc.gpsimd.tensor_scalar(out=whole[:], in0=turns[:], scalar1=1.0, scalar2=0.0, op0=ALU.mult, op1=ALU.add)
        neg_ident = keep.tile([P, P], F32, name="neg_ident")
        nc.gpsimd.tensor_scalar(out=neg_ident[:], in0=ident[:], scalar1=-1.0, scalar2=0.0, op0=ALU.mult, op1=ALU.add)
        two_pi = 2.0 * math.pi

        def fold(c):
            rows = slice(c * SLOTS, (c + 1) * SLOTS)
            nc.vector.tensor_tensor(out=frac[:, :, rows, :], in0=turns[:, :, rows, :], in1=whole[:, :, rows, :], op=ALU.subtract)
            nc.vector.scalar_tensor_tensor(
                out=negf[:, :, rows, :], in0=frac[:, :, rows, :], scalar=0.5, in1=frac[:, :, rows, :],
                op0=ALU.is_gt, op1=ALU.subtract,
            )

        def sines(c):
            rows = slice(c * SLOTS, (c + 1) * SLOTS)
            for src, e, which, scale in ((0, 0, 0, -two_pi), (0, 1, 1, -two_pi), (1, 0, 1, two_pi), (1, 1, 0, -two_pi)):
                nc.scalar.activation(
                    out=tab[:, rows, src, :].rearrange("p s (d e j) -> p s d e j", d=2, e=2)[:, :, :, e, :],
                    in_=negf[:, which, rows, :].rearrange("p s (d j) -> p s d j", d=2),
                    func=ACT.Sin, scale=scale,
                )

        u_codes = keep.tile([P, 16, 256], U32, name="u_codes", align_bytes=64)
        u_scales = keep.tile([P, 16, 256], U8, name="u_scales", align_bytes=64)
        w_codes = keep.tile([P, 2, 2, 512], U32, name="w_codes", align_bytes=64)
        w_scales = keep.tile([P, 2, 2, 512], U8, name="w_scales", align_bytes=64)
        w_grouped = []
        for nh in range(2):
            wg = keep.tile([P, 2, 512, 4], BF16, name="wg%d" % nh, align_bytes=64)
            w_grouped.append(wg)
        u_grouped = {}

        sorted_tiles = {}

        def sort_words(kind, idx, on_vector):
            words = w_words[idx] if kind == "w" else u_words[idx]
            sorted_words = stage.tile([P, 2, 2, P], F32, name="sorted_words", bufs=4)
            src = words.rearrange("p (g w u) -> p g u w", g=2, u=2)
            if on_vector:
                nc.vector.tensor_copy(out=sorted_words[:], in_=src)
            else:
                nc.scalar.copy(out=sorted_words[:], in_=src)
            sorted_tiles[(kind, idx)] = sorted_words

        def front(kind, idx):
            words = w_words[idx] if kind == "w" else u_words[idx]
            xt = psum_t.tile([P, 2, 2, P], F32, name="xt")
            mat = perm if kind == "w" else ident
            for g in range(2):
                for u in range(2):
                    if (kind, idx) in sorted_tiles:
                        nc.tensor.transpose(xt[:, g, u, :], sorted_tiles[(kind, idx)][:, g, u, :], mat[:])
                    else:
                        nc.tensor.transpose(xt[:, g, u, :], words[:, 256 * g + u:256 * (g + 1):2], mat[:])
            if kind == "w":
                lo = (idx % 4) * 64
                for g in range(2):
                    nc.scalar.copy(
                        out=w_grouped[idx // 4][:].bitcast(F32)[:, g].rearrange("p (s n) u -> p s n u", s=2)[:, :, lo:lo + 64, :],
                        in_=xt[:, g].rearrange("p u (s c) -> p s c u", s=2),
                    )
            else:
                q, t = divmod(idx, SLOTS)
                if t == 0:
                    ug = stage.tile([P, SLOTS, 2, P, 4], BF16, name="ug", align_bytes=64, bufs=2)
                    u_grouped[q] = ug
                nc.scalar.copy(out=u_grouped[q][:, t].bitcast(F32), in_=xt[:].rearrange("p g u r -> p g r u"))

        def w_quant(nh, g0, n):
            nc.vector.quantize_mx(
                out=w_codes[:, nh, g0:g0 + n, :].rearrange("p g n -> p (g n)").bitcast(FP8X4),
                scales=w_scales[:, nh, g0:g0 + n, :].rearrange("p g n -> p (g n)"),
                in_=w_grouped[nh][:, g0:g0 + n].rearrange("p g n j -> p (g n j)"),
            )

        def u_quant(i, n):
            q, t = divmod(i, SLOTS)
            nc.vector.quantize_mx(
                out=u_codes[:, i:i + n, :].rearrange("p i c -> p (i c)").bitcast(FP8X4),
                scales=u_scales[:, i:i + n, :].rearrange("p i c -> p (i c)"),
                in_=u_grouped[q][:, t:t + n].rearrange("p t g r j -> p (t g r j)"),
            )

        def product(i, nh, side=False):
            if side:
                bank = psum_t.tile([P, 2, 2, P], F32, name="xt")
                acc = bank[:].rearrange("p a b c -> p (a b c)")
            else:
                bank = psum_a.tile([P, 512], F32, name="acc")
                acc = bank[:]
            for g in range(2):
                cols = slice(g * P, (g + 1) * P)
                nc.tensor.matmul_mx(
                    out=acc,
                    lhsT=u_codes[:, i, cols].bitcast(FP8X4), lhsT_scale=u_scales[:, i, cols],
                    rhs=w_codes[:, nh, g, :].bitcast(FP8X4), rhs_scale=w_scales[:, nh, g, :],
                    start=(g == 0), stop=(g == 1),
                )
            return acc

        def multiply(acc, ts, pr_k):
            shape = [P, 2, 8, 2, 2, 16]
            nc.vector.tensor_tensor(
                out=pr_k.rearrange("p s (h d e j) -> p s h d e j", h=8, d=2, e=2),
                in0=acc.rearrange("p (s h d j) -> p s h d j", s=2, h=8, d=2).unsqueeze(4).to_broadcast(shape),
                in1=tab[:, ts].rearrange("p s (d e j) -> p s d e j", d=2, e=2).unsqueeze(2).to_broadcast(shape),
                op=ALU.mult,
            )

        def add(engine, pr, res, t0, n, heads=slice(0, 8)):
            engine.tensor_tensor(
                out=res[:, heads, t0:t0 + n, :].rearrange("p h t c -> p t h c"),
                in0=pr[:, 0:n, 0, :].rearrange("p k (h c) -> p k h c", h=8)[:, :, heads, :],
                in1=pr[:, 0:n, 1, :].rearrange("p k (h c) -> p k h c", h=8)[:, :, heads, :],
                op=ALU.add,
            )

        for kind, idx in HEAD_TILES:
            sort_words(kind, idx, True)
            front(kind, idx)
        u_quant(0, 1)
        fold(0)
        front("u", 1)
        sines(0)
        w_quant(0, 0, 1)
        w_quant(0, 1, 1)
        u_quant(1, 1)
        fold(1)
        front("u", 2)
        u_quant(2, 1)

        sorts = {}
        fronts = {}
        quants = {0: [("u", 3, 1)], 13: [("w", 1, 2)]}
        fronts[0] = [("u", 3)]
        for n in range(4, 16):
            fronts.setdefault(n - FRONT_LEAD, []).append(("u", n))
            if n % 2 == 0:
                quants.setdefault(n - QUANT_LEAD, []).append(("u", n, 2))
        for k in range(4):
            fronts.setdefault(4 + 3 * k, []).append(("w", 4 + k))

        y2 = stage.tile([P, 32, 2, 2, 8], F32, name="y2", bufs=1)
        prod = stage.tile([P, 2, 2, 2, 16, 16], F32, name="prod", bufs=1)

        def side_gather(accs):
            for b in range(2):
                nc.scalar.copy(out=y2[:, :, :, b, :], in_=accs[b].rearrange("p (s h x) -> p x s h", s=2, h=8))

        def side_rotate(lo, hi):
            for x in range(lo, hi):
                d, j = divmod(x, 16)
                for kind in range(2):
                    col = 32 * d + 16 * kind + j
                    nc.scalar.activation(
                        out=prod[:, kind, :, d, j, :], in_=y2[:, x].rearrange("p s b h -> p s (b h)"),
                        func=ACT.Copy, scale=tab[:, SIDE_SLOT, 0, col:col + 1],
                    )

        low_res = stage.tile([P, 2, 8, 2, DH], F32, name="low_res", bufs=1)

        def side_finish(b, e):
            bank = psum_t.tile([P, 2, 2, P], F32, name="xt")
            heads = slice(8 * b, 8 * b + 8)
            terms = ((neg_ident, 1, 1), (ident, 0, 0)) if e == 0 else ((ident, 0, 1), (ident, 1, 0))
            for n, (mat, kind, s) in enumerate(terms):
                nc.tensor.matmul(
                    out=bank[:, 0].rearrange("p d (j h) -> p d j h", h=8), lhsT=mat[:], rhs=prod[:, kind, s, :, :, heads],
                    start=(n == 0), stop=(n == 1),
                )
            nc.scalar.copy(
                out=low_res[:, b, :, SIDE_SLOT, :].rearrange("p h (d e j) -> p h d e j", d=2, e=2)[:, :, :, e, :],
                in_=bank[:, 0].rearrange("p d (j h) -> p h d j", h=8),
            )
            if e == 1:
                dst = out[b, 8:16, :, :].rearrange("h (p s) c -> p h s c", s=2 * SLOTS)
                nc.sync.dma_start(out=dst[:, :, 0:2, :], in_=low_res[:, b])

        res = None
        pr = None
        for s in range(16):
            q, t = divmod(s, 4)
            b, c = q // 2, q % 2
            group = 1 if s < 2 else PAIR
            acc = product(s, 0)
            for kind, idx in fronts.get(s, []):
                front(kind, idx)
            if s == 2:
                sines(1)
            if t == 0:
                res = stage.tile([P, 8, SLOTS, DH], F32, name="res")
            if t % group == 0:
                pr = stage.tile([P, PAIR, 2, 512], F32, name="pr", bufs=4)
            multiply(acc, c * SLOTS + t, pr[:, t % group])
            for kind, idx, n in quants.get(s, []):
                if kind == "u":
                    u_quant(idx, n)
                else:
                    w_quant(idx, 0, n)
            dst = out[b, 0:8, :, :].rearrange("h (p s) c -> p h s c", s=2 * SLOTS)
            if t % group == group - 1:
                add(nc.gpsimd, pr, res, t - group + 1, group)
            if t == SLOTS - 1:
                nc.sync.dma_start(out=dst[:, :, c * SLOTS:(c + 1) * SLOTS, :], in_=res[:])

        side_gather([product(8 * b + SIDE_SLOT, 1, True) for b in range(2)])
        side_rotate(0, 32)
        k = 0
        for tiles in MAIN_GROUPS:
            pr = stage.tile([P, PAIR, 2, 512], F32, name="pr", bufs=4)
            q, t0 = divmod(tiles[0], 4)
            b, c = q // 2, q % 2
            if t0 == 0 or (c == 0 and t0 == 2):
                res = stage.tile([P, 8, SLOTS, DH], F32, name="res")
            for m, i in enumerate(tiles):
                acc = product(i, 1)
                if k in SIDE_ADDS:
                    side_finish(SIDE_ADDS[k][0], SIDE_ADDS[k][1])
                multiply(acc, i % 8, pr[:, m])
                k += 1
            if t0 == 1:
                nc.gpsimd.tensor_tensor(
                    out=low_res[:, :, :, 1, :],
                    in0=pr[:, :, 0, :].rearrange("p k (h c) -> p k h c", h=8),
                    in1=pr[:, :, 1, :].rearrange("p k (h c) -> p k h c", h=8),
                    op=ALU.add,
                )
                continue
            dst = out[b, 8:16, :, :].rearrange("h (p s) c -> p h s c", s=2 * SLOTS)
            if q == 3:
                for heads in (slice(0, 4), slice(4, 8)):
                    add(nc.vector if tiles[-1] == 15 else nc.gpsimd, pr, res, t0, 2, heads)
                    nc.sync.dma_start(out=dst[:, heads, c * SLOTS + t0:c * SLOTS + t0 + 2, :], in_=res[:, heads, t0:t0 + 2, :])
                continue
            add(nc.gpsimd, pr, res, t0, 2)
            if c == 0:
                nc.sync.dma_start(out=dst[:, :, c * SLOTS + t0:c * SLOTS + t0 + 2, :], in_=res[:, :, t0:t0 + 2, :])
            elif t0 == 2:
                nc.sync.dma_start(out=dst[:, :, c * SLOTS:(c + 1) * SLOTS, :], in_=res[:])
